import numpy as np
import ml_dtypes


def mxq(x, axis, fmt="e4m3"):
    dtype, down = {"e4m3": (ml_dtypes.float8_e4m3fn, 7), "e5m2": (ml_dtypes.float8_e5m2, 14)}[fmt]
    v = np.moveaxis(np.asarray(x, np.float32).astype(ml_dtypes.bfloat16).astype(np.float64), axis, -1)
    blocks = v.reshape(v.shape[:-1] + (-1, 32))
    amax = np.abs(blocks).max(-1, keepdims=True)
    byte = np.maximum(np.where(amax > 0, np.frexp(amax)[1] - 1 + 127, 0) - down, 1)
    scale = np.exp2(byte - 127.0)
    codes = (blocks / scale).astype(np.float32).astype(dtype).astype(np.float64)
    return np.moveaxis((codes * scale).reshape(v.shape), -1, axis)


WIDE = False


def mx_kscale(k):
    if not WIDE:
        return np.ones(k)
    levels = np.array([10, -10, 5, -5, 0])
    a = np.random.permutation(np.resize(levels, k // 512 * 4)).reshape(k // 512, 4)
    idx = np.arange(k)
    return np.exp2(a[idx // 512, idx % 128 // 32])


BF16 = ml_dtypes.bfloat16


def bf(x):
    return np.asarray(x, np.float32).astype(BF16)


def f64(x):
    return np.asarray(x).astype(np.float64)


B, S, D, E, Q = 32, 256, 512, 512, 128
P = S - Q


def setup_inputs():
    s = mx_kscale(E)
    return {"q_rot": bf(np.random.standard_normal((B, Q, E)) * s),
            "k_rot": bf(np.random.standard_normal((B, S, E)) / s)}


def reference(q_rot, k_rot):
    scores = (mxq(f64(q_rot), 2, "e4m3") @ mxq(f64(k_rot), 2, "e4m3").transpose(0, 2, 1)) / np.sqrt(E)
    mask = np.triu(np.full((Q, S), -np.inf), 1 + P)
    scores = scores + mask
    e = np.exp(scores - scores.max(-1, keepdims=True))
    return e / e.sum(-1, keepdims=True)

@@ -1,0 +1,152 @@
+from contextlib import ExitStack
+import math
+
+import concourse.mybir as mybir
+from concourse.masks import make_identity
+
+F32 = mybir.dt.float32
+BF16 = mybir.dt.bfloat16
+U32 = mybir.dt.uint32
+U8 = mybir.dt.uint8
+FP8X4 = mybir.dt.float8_e4m3fn_x4
+ALU = mybir.AluOpType
+ACT = mybir.ActivationFunctionType
+
+P = 128
+B, Q, S, E = 32, 128, 256, 512
+FIRST_POSITION = S - Q
+PAIR = 2
+N_PAIRS = B // PAIR
+ROWS = 2
+WORDS = E // 2
+HALVES = WORDS // P
+SLOTS = ROWS * HALVES
+BLOCK = P * ROWS
+MASKED = -1.0e30
+SCALE = 1.0 / math.sqrt(E)
+
+FLOPS = 2 * B * Q * S * E
+
+
+def transpose_block(nc, banks, raw_words, identity, grouped_words):
+    bank = banks.tile([P, SLOTS, P], F32)
+    for slot in range(SLOTS):
+        nc.tensor.transpose(bank[:, slot, :], raw_words[:, slot * P : (slot + 1) * P], identity)
+    nc.scalar.copy(
+        out=grouped_words.rearrange("p (c s) -> p c s", s=SLOTS),
+        in_=bank[:].rearrange("p s c -> p c s"),
+    )
+
+
+def tile_rawattention_pb_t_kernel(tc, q_rot, k_rot, out):
+    nc = tc.nc
+    q_blocks = q_rot.flatten_outer_dims().rearrange("(g c t) e -> g c (t e)", c=P, t=ROWS)
+    k_blocks = k_rot.flatten_outer_dims().rearrange(
+        "(g h c t) e -> g c h (t e)", h=PAIR, c=P, t=ROWS
+    )
+    out_pairs = out.rearrange("(g h) i j -> g i h j", h=PAIR)
+
+    with ExitStack() as ctx:
+        const = ctx.enter_context(tc.tile_pool(name="const", bufs=1))
+        raw = ctx.enter_context(tc.tile_pool(name="raw", bufs=N_PAIRS))
+        work = ctx.enter_context(tc.tile_pool(name="work", bufs=3))
+        result = ctx.enter_context(tc.tile_pool(name="result", bufs=N_PAIRS))
+        banks = ctx.enter_context(tc.psum_pool(name="banks", bufs=6))
+        score_banks = ctx.enter_context(tc.psum_pool(name="score_banks", bufs=2))
+
+        q_raws = []
+        k_raws = []
+        for g in range(N_PAIRS):
+            q_raw = raw.tile([P, ROWS * E], BF16)
+            nc.sync.dma_start(out=q_raw[:], in_=q_blocks[g])
+            k_raw = raw.tile([P, PAIR, ROWS * E], BF16)
+            nc.sync.dma_start(out=k_raw[:], in_=k_blocks[g])
+            q_raws.append(q_raw)
+            k_raws.append(k_raw)
+
+        identity = const.tile([P, P], F32)
+        make_identity(nc, identity[:])
+
+        mask = const.tile([P, PAIR, S], F32)
+        nc.gpsimd.memset(mask[:], 0.0)
+        for h in range(PAIR):
+            nc.gpsimd.affine_select(
+                out=mask[:, h, :],
+                in_=mask[:, h, :],
+                compare_op=ALU.is_ge,
+                fill=MASKED,
+                base=FIRST_POSITION,
+                pattern=[[-1, S]],
+                channel_multiplier=1,
+            )
+
+        zero = const.tile([P, 1], F32)
+        nc.vector.memset(zero[:], 0.0)
+        one = const.tile([P, 1], F32)
+        nc.scalar.activation(out=one[:], in_=zero[:], func=ACT.Exp)
+
+        for g in range(N_PAIRS):
+            q_grouped = work.tile([P, BLOCK * 4], BF16, align_bytes=64)
+            k_grouped = work.tile([P, PAIR * BLOCK * 4], BF16, align_bytes=64)
+            transpose_block(
+                nc, banks, q_raws[g][:].bitcast(F32), identity[:], q_grouped[:].bitcast(F32)
+            )
+            for h in range(PAIR):
+                transpose_block(
+                    nc,
+                    banks,
+                    k_raws[g][:, h, :].bitcast(F32),
+                    identity[:],
+                    k_grouped[:, h * BLOCK * 4 : (h + 1) * BLOCK * 4].bitcast(F32),
+                )
+
+            q_codes = work.tile([P, BLOCK], U32, align_bytes=64)
+            q_scales = work.tile([P, BLOCK], U8, align_bytes=64)
+            nc.vector.quantize_mx(out=q_codes[:].bitcast(FP8X4), scales=q_scales[:], in_=q_grouped[:])
+            k_codes = work.tile([P, PAIR * BLOCK], U32, align_bytes=64)
+            k_scales = work.tile([P, PAIR * BLOCK], U8, align_bytes=64)
+            nc.vector.quantize_mx(out=k_codes[:].bitcast(FP8X4), scales=k_scales[:], in_=k_grouped[:])
+
+            scores = score_banks.tile([P, PAIR, S], F32)
+            for h in range(PAIR):
+                nc.tensor.matmul_mx(
+                    out=scores[:, h, :],
+                    lhsT=q_codes[:, h * Q : (h + 1) * Q].bitcast(FP8X4),
+                    lhsT_scale=q_scales[:, h * Q : (h + 1) * Q],
+                    rhs=k_codes[:, h * S : (h + 1) * S].bitcast(FP8X4),
+                    rhs_scale=k_scales[:, h * S : (h + 1) * S],
+                    start=True,
+                    stop=True,
+                )
+
+            logits = work.tile([P, PAIR, S], F32)
+            nc.vector.scalar_tensor_tensor(
+                out=logits[:], in0=scores[:], scalar=SCALE, in1=mask[:], op0=ALU.mult, op1=ALU.add
+            )
+            minus_max = work.tile([P, PAIR], F32)
+            nc.vector.tensor_reduce(
+                out=minus_max[:], in_=logits[:], axis=mybir.AxisListType.X, op=ALU.max, negate=True
+            )
+            weights = work.tile([P, PAIR, S], F32)
+            sums = work.tile([P, PAIR], F32)
+            for h in range(PAIR):
+                nc.scalar.activation(
+                    out=weights[:, h, :],
+                    in_=logits[:, h, :],
+                    func=ACT.Exp,
+                    bias=minus_max[:, h : h + 1],
+                    scale=1.0,
+                    accum_out=sums[:, h : h + 1],
+                )
+            inverse = work.tile([P, PAIR], F32)
+            nc.vector.reciprocal(out=inverse[:], in_=sums[:])
+            probs = result.tile([P, PAIR, S], F32)
+            for h in range(PAIR):
+                nc.vector.tensor_scalar(
+                    out=probs[:, h, :],
+                    in0=weights[:, h, :],
+                    scalar1=inverse[:, h : h + 1],
+                    scalar2=None,
+                    op0=ALU.mult,
+                )
+            nc.sync.dma_start(out=out_pairs[g], in_=probs[:])

@@ -18,51 +18,38 @@ FIRST_POSITION = S - Q
 PAIR = 2
 N_PAIRS = B // PAIR
 ROWS = 2
-WORDS = E // 2
-HALVES = WORDS // P
-SLOTS = ROWS * HALVES
 BLOCK = P * ROWS
+WORDS = E // 2
+SLOTS = ROWS * WORDS // P
+PACK = 4
+N_BLOCKS = 3
+K_COLS = PAIR * S
 MASKED = -1.0e30
 SCALE = 1.0 / math.sqrt(E)
 
 FLOPS = 2 * B * Q * S * E
 
 
-def transpose_block(nc, banks, raw_words, identity, grouped_words):
-    bank = banks.tile([P, SLOTS, P], F32)
-    for slot in range(SLOTS):
-        nc.tensor.transpose(bank[:, slot, :], raw_words[:, slot * P : (slot + 1) * P], identity)
-    nc.scalar.copy(
-        out=grouped_words.rearrange("p (c s) -> p c s", s=SLOTS),
-        in_=bank[:].rearrange("p s c -> p c s"),
-    )
-
-
 def tile_rawattention_pb_t_kernel(tc, q_rot, k_rot, out):
     nc = tc.nc
-    q_blocks = q_rot.flatten_outer_dims().rearrange("(g c t) e -> g c (t e)", c=P, t=ROWS)
-    k_blocks = k_rot.flatten_outer_dims().rearrange(
-        "(g h c t) e -> g c h (t e)", h=PAIR, c=P, t=ROWS
-    )
+    q_blocks = q_rot.flatten_outer_dims().rearrange("(n c t) e -> n c (t e)", c=P, t=ROWS)
+    k_blocks = k_rot.flatten_outer_dims().rearrange("(n c t) e -> n c (t e)", c=P, t=ROWS)
     out_pairs = out.rearrange("(g h) i j -> g i h j", h=PAIR)
 
     with ExitStack() as ctx:
         const = ctx.enter_context(tc.tile_pool(name="const", bufs=1))
-        raw = ctx.enter_context(tc.tile_pool(name="raw", bufs=N_PAIRS))
+        raw = ctx.enter_context(tc.tile_pool(name="raw", bufs=N_PAIRS * N_BLOCKS))
         work = ctx.enter_context(tc.tile_pool(name="work", bufs=3))
         result = ctx.enter_context(tc.tile_pool(name="result", bufs=N_PAIRS))
-        banks = ctx.enter_context(tc.psum_pool(name="banks", bufs=6))
+        banks = ctx.enter_context(tc.psum_pool(name="banks", bufs=2 * N_BLOCKS))
         score_banks = ctx.enter_context(tc.psum_pool(name="score_banks", bufs=2))
 
-        q_raws = []
-        k_raws = []
+        raw_blocks = []
         for g in range(N_PAIRS):
-            q_raw = raw.tile([P, ROWS * E], BF16)
-            nc.sync.dma_start(out=q_raw[:], in_=q_blocks[g])
-            k_raw = raw.tile([P, PAIR, ROWS * E], BF16)
-            nc.sync.dma_start(out=k_raw[:], in_=k_blocks[g])
-            q_raws.append(q_raw)
-            k_raws.append(k_raw)
+            for block in (k_blocks[PAIR * g], k_blocks[PAIR * g + 1], q_blocks[g]):
+                raw_block = raw.tile([P, ROWS * E], BF16)
+                nc.sync.dma_start(out=raw_block[:], in_=block)
+                raw_blocks.append(raw_block)
 
         identity = const.tile([P, P], F32)
         make_identity(nc, identity[:])
@@ -85,68 +72,121 @@ def tile_rawattention_pb_t_kernel(tc, q_rot, k_rot, out):
         one = const.tile([P, 1], F32)
         nc.scalar.activation(out=one[:], in_=zero[:], func=ACT.Exp)
 
-        for g in range(N_PAIRS):
-            q_grouped = work.tile([P, BLOCK * 4], BF16, align_bytes=64)
-            k_grouped = work.tile([P, PAIR * BLOCK * 4], BF16, align_bytes=64)
-            transpose_block(
-                nc, banks, q_raws[g][:].bitcast(F32), identity[:], q_grouped[:].bitcast(F32)
-            )
-            for h in range(PAIR):
-                transpose_block(
-                    nc,
-                    banks,
-                    k_raws[g][:, h, :].bitcast(F32),
-                    identity[:],
-                    k_grouped[:, h * BLOCK * 4 : (h + 1) * BLOCK * 4].bitcast(F32),
+        transposed = {}
+        grouped = {}
+        operands = {}
+        scores = {}
+        logits = {}
+        weights = {}
+
+        def transpose(g):
+            transposed[g] = []
+            for n in range(N_BLOCKS):
+                words = raw_blocks[N_BLOCKS * g + n][:].bitcast(F32)
+                bank = banks.tile([P, SLOTS, P], F32)
+                for slot in range(SLOTS):
+                    nc.tensor.transpose(
+                        bank[:, slot, :], words[:, slot * P : (slot + 1) * P], identity[:]
+                    )
+                transposed[g].append(bank)
+
+        def regroup(g):
+            rows = work.tile([P, N_BLOCKS * BLOCK * PACK], BF16, align_bytes=64)
+            for n in range(N_BLOCKS):
+                nc.scalar.copy(
+                    out=rows[:, n * BLOCK * PACK : (n + 1) * BLOCK * PACK]
+                    .bitcast(F32)
+                    .rearrange("p (c s) -> p c s", s=SLOTS),
+                    in_=transposed[g][n][:].rearrange("p s c -> p c s"),
                 )
+            grouped[g] = rows
 
-            q_codes = work.tile([P, BLOCK], U32, align_bytes=64)
-            q_scales = work.tile([P, BLOCK], U8, align_bytes=64)
-            nc.vector.quantize_mx(out=q_codes[:].bitcast(FP8X4), scales=q_scales[:], in_=q_grouped[:])
-            k_codes = work.tile([P, PAIR * BLOCK], U32, align_bytes=64)
-            k_scales = work.tile([P, PAIR * BLOCK], U8, align_bytes=64)
-            nc.vector.quantize_mx(out=k_codes[:].bitcast(FP8X4), scales=k_scales[:], in_=k_grouped[:])
+        def quantise(g):
+            codes = work.tile([P, N_BLOCKS * BLOCK], U32, align_bytes=64)
+            scales = work.tile([P, N_BLOCKS * BLOCK], U8, align_bytes=64)
+            for first, last in ((0, K_COLS), (K_COLS, N_BLOCKS * BLOCK)):
+                nc.vector.quantize_mx(
+                    out=codes[:, first:last].bitcast(FP8X4),
+                    scales=scales[:, first:last],
+                    in_=grouped[g][:, first * PACK : last * PACK],
+                )
+            operands[g] = (codes, scales)
 
-            scores = score_banks.tile([P, PAIR, S], F32)
+        def multiply(g):
+            codes, scales = operands[g]
+            bank = score_banks.tile([P, PAIR, S], F32)
             for h in range(PAIR):
+                q_cols = slice(K_COLS + h * Q, K_COLS + (h + 1) * Q)
+                k_cols = slice(h * S, (h + 1) * S)
                 nc.tensor.matmul_mx(
-                    out=scores[:, h, :],
-                    lhsT=q_codes[:, h * Q : (h + 1) * Q].bitcast(FP8X4),
-                    lhsT_scale=q_scales[:, h * Q : (h + 1) * Q],
-                    rhs=k_codes[:, h * S : (h + 1) * S].bitcast(FP8X4),
-                    rhs_scale=k_scales[:, h * S : (h + 1) * S],
+                    out=bank[:, h, :],
+                    lhsT=codes[:, q_cols].bitcast(FP8X4),
+                    lhsT_scale=scales[:, q_cols],
+                    rhs=codes[:, k_cols].bitcast(FP8X4),
+                    rhs_scale=scales[:, k_cols],
                     start=True,
                     stop=True,
                 )
+            scores[g] = bank
 
-            logits = work.tile([P, PAIR, S], F32)
+        def mask_and_max(g):
+            masked = work.tile([P, PAIR, S], F32)
             nc.vector.scalar_tensor_tensor(
-                out=logits[:], in0=scores[:], scalar=SCALE, in1=mask[:], op0=ALU.mult, op1=ALU.add
+                out=masked[:], in0=scores[g][:], scalar=SCALE, in1=mask[:], op0=ALU.mult, op1=ALU.add
             )
             minus_max = work.tile([P, PAIR], F32)
             nc.vector.tensor_reduce(
-                out=minus_max[:], in_=logits[:], axis=mybir.AxisListType.X, op=ALU.max, negate=True
+                out=minus_max[:], in_=masked[:], axis=mybir.AxisListType.X, op=ALU.max, negate=True
             )
-            weights = work.tile([P, PAIR, S], F32)
+            logits[g] = (masked, minus_max)
+
+        def exponentials(g):
+            masked, minus_max = logits[g]
+            exps = work.tile([P, PAIR, S], F32)
             sums = work.tile([P, PAIR], F32)
             for h in range(PAIR):
                 nc.scalar.activation(
-                    out=weights[:, h, :],
-                    in_=logits[:, h, :],
+                    out=exps[:, h, :],
+                    in_=masked[:, h, :],
                     func=ACT.Exp,
                     bias=minus_max[:, h : h + 1],
                     scale=1.0,
                     accum_out=sums[:, h : h + 1],
                 )
+            weights[g] = (exps, sums)
+
+        def normalise_and_store(g):
+            exps, sums = weights[g]
             inverse = work.tile([P, PAIR], F32)
             nc.vector.reciprocal(out=inverse[:], in_=sums[:])
             probs = result.tile([P, PAIR, S], F32)
             for h in range(PAIR):
-                nc.vector.tensor_scalar(
+                nc.gpsimd.tensor_scalar(
                     out=probs[:, h, :],
-                    in0=weights[:, h, :],
+                    in0=exps[:, h, :],
                     scalar1=inverse[:, h : h + 1],
-                    scalar2=None,
+                    scalar2=0.0,
                     op0=ALU.mult,
+                    op1=ALU.add,
                 )
             nc.sync.dma_start(out=out_pairs[g], in_=probs[:])
+
+        def exists(g):
+            return 0 <= g < N_PAIRS
+
+        with tc.manual_schedule():
+            for step in range(-1, N_PAIRS + 3):
+                if exists(step - 2):
+                    mask_and_max(step - 2)
+                if exists(step - 1):
+                    multiply(step - 1)
+                if exists(step + 1):
+                    transpose(step + 1)
+                if exists(step):
+                    regroup(step)
+                if exists(step - 2):
+                    exponentials(step - 2)
+                if exists(step):
+                    quantise(step)
+                if exists(step - 3):
+                    normalise_and_store(step - 3)

@@ -24,6 +24,7 @@ SLOTS = ROWS * WORDS // P
 PACK = 4
 N_BLOCKS = 3
 K_COLS = PAIR * S
+VECTOR_EVERY = 4
 MASKED = -1.0e30
 SCALE = 1.0 / math.sqrt(E)
 
@@ -34,12 +35,11 @@ def tile_rawattention_pb_t_kernel(tc, q_rot, k_rot, out):
     nc = tc.nc
     q_blocks = q_rot.flatten_outer_dims().rearrange("(n c t) e -> n c (t e)", c=P, t=ROWS)
     k_blocks = k_rot.flatten_outer_dims().rearrange("(n c t) e -> n c (t e)", c=P, t=ROWS)
-    out_pairs = out.rearrange("(g h) i j -> g i h j", h=PAIR)
 
     with ExitStack() as ctx:
         const = ctx.enter_context(tc.tile_pool(name="const", bufs=1))
         raw = ctx.enter_context(tc.tile_pool(name="raw", bufs=N_PAIRS * N_BLOCKS))
-        work = ctx.enter_context(tc.tile_pool(name="work", bufs=3))
+        work = ctx.enter_context(tc.tile_pool(name="work", bufs=4))
         result = ctx.enter_context(tc.tile_pool(name="result", bufs=N_PAIRS))
         banks = ctx.enter_context(tc.psum_pool(name="banks", bufs=2 * N_BLOCKS))
         score_banks = ctx.enter_context(tc.psum_pool(name="score_banks", bufs=2))
@@ -77,6 +77,7 @@ def tile_rawattention_pb_t_kernel(tc, q_rot, k_rot, out):
         operands = {}
         scores = {}
         logits = {}
+        shifts = {}
         weights = {}
 
         def transpose(g):
@@ -93,7 +94,9 @@ def tile_rawattention_pb_t_kernel(tc, q_rot, k_rot, out):
         def regroup(g):
             rows = work.tile([P, N_BLOCKS * BLOCK * PACK], BF16, align_bytes=64)
             for n in range(N_BLOCKS):
-                nc.scalar.copy(
+                to_vector = n == N_BLOCKS - 1 and g % VECTOR_EVERY == 0
+                copy_out = nc.vector.tensor_copy if to_vector else nc.scalar.copy
+                copy_out(
                     out=rows[:, n * BLOCK * PACK : (n + 1) * BLOCK * PACK]
                     .bitcast(F32)
                     .rearrange("p (c s) -> p c s", s=SLOTS),
@@ -129,19 +132,22 @@ def tile_rawattention_pb_t_kernel(tc, q_rot, k_rot, out):
                 )
             scores[g] = bank
 
-        def mask_and_max(g):
+        def mask_scores(g):
             masked = work.tile([P, PAIR, S], F32)
             nc.vector.scalar_tensor_tensor(
                 out=masked[:], in0=scores[g][:], scalar=SCALE, in1=mask[:], op0=ALU.mult, op1=ALU.add
             )
+            logits[g] = masked
+
+        def row_maxima(g):
             minus_max = work.tile([P, PAIR], F32)
             nc.vector.tensor_reduce(
-                out=minus_max[:], in_=masked[:], axis=mybir.AxisListType.X, op=ALU.max, negate=True
+                out=minus_max[:], in_=logits[g][:], axis=mybir.AxisListType.X, op=ALU.max, negate=True
             )
-            logits[g] = (masked, minus_max)
+            shifts[g] = minus_max
 
         def exponentials(g):
-            masked, minus_max = logits[g]
+            masked, minus_max = logits[g], shifts[g]
             exps = work.tile([P, PAIR, S], F32)
             sums = work.tile([P, PAIR], F32)
             for h in range(PAIR):
@@ -160,8 +166,9 @@ def tile_rawattention_pb_t_kernel(tc, q_rot, k_rot, out):
             inverse = work.tile([P, PAIR], F32)
             nc.vector.reciprocal(out=inverse[:], in_=sums[:])
             probs = result.tile([P, PAIR, S], F32)
+            divider = nc.vector if g == N_PAIRS - 1 else nc.gpsimd
             for h in range(PAIR):
-                nc.gpsimd.tensor_scalar(
+                divider.tensor_scalar(
                     out=probs[:, h, :],
                     in0=exps[:, h, :],
                     scalar1=inverse[:, h : h + 1],
@@ -169,24 +176,26 @@ def tile_rawattention_pb_t_kernel(tc, q_rot, k_rot, out):
                     op0=ALU.mult,
                     op1=ALU.add,
                 )
-            nc.sync.dma_start(out=out_pairs[g], in_=probs[:])
+                nc.sync.dma_start(out=out[PAIR * g + h], in_=probs[:, h, :])
 
         def exists(g):
             return 0 <= g < N_PAIRS
 
         with tc.manual_schedule():
-            for step in range(-1, N_PAIRS + 3):
-                if exists(step - 2):
-                    mask_and_max(step - 2)
+            for step in range(-1, N_PAIRS + 5):
                 if exists(step - 1):
-                    multiply(step - 1)
+                    quantise(step - 1)
+                if exists(step - 5):
+                    normalise_and_store(step - 5)
                 if exists(step + 1):
                     transpose(step + 1)
+                if exists(step - 1):
+                    multiply(step - 1)
+                if exists(step - 3):
+                    row_maxima(step - 3)
+                if exists(step - 2):
+                    mask_scores(step - 2)
                 if exists(step):
                     regroup(step)
-                if exists(step - 2):
-                    exponentials(step - 2)
-                if exists(step):
-                    quantise(step)
-                if exists(step - 3):
-                    normalise_and_store(step - 3)
+                if exists(step - 4):
+                    exponentials(step - 4)

@@ -24,6 +24,7 @@ SLOTS = ROWS * WORDS // P
 PACK = 4
 N_BLOCKS = 3
 K_COLS = PAIR * S
+PASS_REPEATS = 2
 VECTOR_EVERY = 4
 MASKED = -1.0e30
 SCALE = 1.0 / math.sqrt(E)
@@ -118,18 +119,19 @@ def tile_rawattention_pb_t_kernel(tc, q_rot, k_rot, out):
         def multiply(g):
             codes, scales = operands[g]
             bank = score_banks.tile([P, PAIR, S], F32)
-            for h in range(PAIR):
-                q_cols = slice(K_COLS + h * Q, K_COLS + (h + 1) * Q)
-                k_cols = slice(h * S, (h + 1) * S)
-                nc.tensor.matmul_mx(
-                    out=bank[:, h, :],
-                    lhsT=codes[:, q_cols].bitcast(FP8X4),
-                    lhsT_scale=scales[:, q_cols],
-                    rhs=codes[:, k_cols].bitcast(FP8X4),
-                    rhs_scale=scales[:, k_cols],
-                    start=True,
-                    stop=True,
-                )
+            for repeat in range(PASS_REPEATS):
+                for h in range(PAIR):
+                    q_cols = slice(K_COLS + h * Q, K_COLS + (h + 1) * Q)
+                    k_cols = slice(h * S, (h + 1) * S)
+                    nc.tensor.matmul_mx(
+                        out=bank[:, h, :],
+                        lhsT=codes[:, q_cols].bitcast(FP8X4),
+                        lhsT_scale=scales[:, q_cols],
+                        rhs=codes[:, k_cols].bitcast(FP8X4),
+                        rhs_scale=scales[:, k_cols],
+                        start=True,
+                        stop=True,
+                    )
             scores[g] = bank
 
         def mask_scores(g):

from contextlib import ExitStack
import math

import concourse.mybir as mybir
from concourse.masks import make_identity

F32 = mybir.dt.float32
BF16 = mybir.dt.bfloat16
U32 = mybir.dt.uint32
U8 = mybir.dt.uint8
FP8X4 = mybir.dt.float8_e4m3fn_x4
ALU = mybir.AluOpType
ACT = mybir.ActivationFunctionType

P = 128
B, Q, S, E = 32, 128, 256, 512
FIRST_POSITION = S - Q
PAIR = 2
N_PAIRS = B // PAIR
ROWS = 2
BLOCK = P * ROWS
WORDS = E // 2
SLOTS = ROWS * WORDS // P
PACK = 4
N_BLOCKS = 3
K_COLS = PAIR * S
PASS_REPEATS = 2
VECTOR_EVERY = 4
MASKED = -1.0e30
SCALE = 1.0 / math.sqrt(E)

FLOPS = 2 * B * Q * S * E


def tile_rawattention_pb_t_kernel(tc, q_rot, k_rot, out):
    nc = tc.nc
    q_blocks = q_rot.flatten_outer_dims().rearrange("(n c t) e -> n c (t e)", c=P, t=ROWS)
    k_blocks = k_rot.flatten_outer_dims().rearrange("(n c t) e -> n c (t e)", c=P, t=ROWS)

    with ExitStack() as ctx:
        const = ctx.enter_context(tc.tile_pool(name="const", bufs=1))
        raw = ctx.enter_context(tc.tile_pool(name="raw", bufs=N_PAIRS * N_BLOCKS))
        work = ctx.enter_context(tc.tile_pool(name="work", bufs=4))
        result = ctx.enter_context(tc.tile_pool(name="result", bufs=N_PAIRS))
        banks = ctx.enter_context(tc.psum_pool(name="banks", bufs=2 * N_BLOCKS))
        score_banks = ctx.enter_context(tc.psum_pool(name="score_banks", bufs=2))

        raw_blocks = []
        for g in range(N_PAIRS):
            for block in (k_blocks[PAIR * g], k_blocks[PAIR * g + 1], q_blocks[g]):
                raw_block = raw.tile([P, ROWS * E], BF16)
                nc.sync.dma_start(out=raw_block[:], in_=block)
                raw_blocks.append(raw_block)

        identity = const.tile([P, P], F32)
        make_identity(nc, identity[:])

        mask = const.tile([P, PAIR, S], F32)
        nc.gpsimd.memset(mask[:], 0.0)
        for h in range(PAIR):
            nc.gpsimd.affine_select(
                out=mask[:, h, :],
                in_=mask[:, h, :],
                compare_op=ALU.is_ge,
                fill=MASKED,
                base=FIRST_POSITION,
                pattern=[[-1, S]],
                channel_multiplier=1,
            )

        zero = const.tile([P, 1], F32)
        nc.vector.memset(zero[:], 0.0)
        one = const.tile([P, 1], F32)
        nc.scalar.activation(out=one[:], in_=zero[:], func=ACT.Exp)

        transposed = {}
        grouped = {}
        operands = {}
        scores = {}
        logits = {}
        shifts = {}
        weights = {}

        def transpose(g):
            transposed[g] = []
            for n in range(N_BLOCKS):
                words = raw_blocks[N_BLOCKS * g + n][:].bitcast(F32)
                bank = banks.tile([P, SLOTS, P], F32)
                for slot in range(SLOTS):
                    nc.tensor.transpose(
                        bank[:, slot, :], words[:, slot * P : (slot + 1) * P], identity[:]
                    )
                transposed[g].append(bank)

        def regroup(g):
            rows = work.tile([P, N_BLOCKS * BLOCK * PACK], BF16, align_bytes=64)
            for n in range(N_BLOCKS):
                to_vector = n == N_BLOCKS - 1 and g % VECTOR_EVERY == 0
                copy_out = nc.vector.tensor_copy if to_vector else nc.scalar.copy
                copy_out(
                    out=rows[:, n * BLOCK * PACK : (n + 1) * BLOCK * PACK]
                    .bitcast(F32)
                    .rearrange("p (c s) -> p c s", s=SLOTS),
                    in_=transposed[g][n][:].rearrange("p s c -> p c s"),
                )
            grouped[g] = rows

        def quantise(g):
            codes = work.tile([P, N_BLOCKS * BLOCK], U32, align_bytes=64)
            scales = work.tile([P, N_BLOCKS * BLOCK], U8, align_bytes=64)
            for first, last in ((0, K_COLS), (K_COLS, N_BLOCKS * BLOCK)):
                nc.vector.quantize_mx(
                    out=codes[:, first:last].bitcast(FP8X4),
                    scales=scales[:, first:last],
                    in_=grouped[g][:, first * PACK : last * PACK],
                )
            operands[g] = (codes, scales)

        def multiply(g):
            codes, scales = operands[g]
            bank = score_banks.tile([P, PAIR, S], F32)
            for repeat in range(PASS_REPEATS):
                for h in range(PAIR):
                    q_cols = slice(K_COLS + h * Q, K_COLS + (h + 1) * Q)
                    k_cols = slice(h * S, (h + 1) * S)
                    nc.tensor.matmul_mx(
                        out=bank[:, h, :],
                        lhsT=codes[:, q_cols].bitcast(FP8X4),
                        lhsT_scale=scales[:, q_cols],
                        rhs=codes[:, k_cols].bitcast(FP8X4),
                        rhs_scale=scales[:, k_cols],
                        start=True,
                        stop=True,
                    )
            scores[g] = bank

        def mask_scores(g):
            masked = work.tile([P, PAIR, S], F32)
            nc.vector.scalar_tensor_tensor(
                out=masked[:], in0=scores[g][:], scalar=SCALE, in1=mask[:], op0=ALU.mult, op1=ALU.add
            )
            logits[g] = masked

        def row_maxima(g):
            minus_max = work.tile([P, PAIR], F32)
            nc.vector.tensor_reduce(
                out=minus_max[:], in_=logits[g][:], axis=mybir.AxisListType.X, op=ALU.max, negate=True
            )
            shifts[g] = minus_max

        def exponentials(g):
            masked, minus_max = logits[g], shifts[g]
            exps = work.tile([P, PAIR, S], F32)
            sums = work.tile([P, PAIR], F32)
            for h in range(PAIR):
                nc.scalar.activation(
                    out=exps[:, h, :],
                    in_=masked[:, h, :],
                    func=ACT.Exp,
                    bias=minus_max[:, h : h + 1],
                    scale=1.0,
                    accum_out=sums[:, h : h + 1],
                )
            weights[g] = (exps, sums)

        def normalise_and_store(g):
            exps, sums = weights[g]
            inverse = work.tile([P, PAIR], F32)
            nc.vector.reciprocal(out=inverse[:], in_=sums[:])
            probs = result.tile([P, PAIR, S], F32)
            divider = nc.vector if g == N_PAIRS - 1 else nc.gpsimd
            for h in range(PAIR):
                divider.tensor_scalar(
                    out=probs[:, h, :],
                    in0=exps[:, h, :],
                    scalar1=inverse[:, h : h + 1],
                    scalar2=0.0,
                    op0=ALU.mult,
                    op1=ALU.add,
                )
                nc.sync.dma_start(out=out[PAIR * g + h], in_=probs[:, h, :])

        def exists(g):
            return 0 <= g < N_PAIRS

        with tc.manual_schedule():
            for step in range(-1, N_PAIRS + 5):
                if exists(step - 1):
                    quantise(step - 1)
                if exists(step - 5):
                    normalise_and_store(step - 5)
                if exists(step + 1):
                    transpose(step + 1)
                if exists(step - 1):
                    multiply(step - 1)
                if exists(step - 3):
                    row_maxima(step - 3)
                if exists(step - 2):
                    mask_scores(step - 2)
                if exists(step):
                    regroup(step)
                if exists(step - 4):
                    exponentials(step - 4)
